import numpy as np
import ml_dtypes


def mxq(x, axis, fmt="e4m3"):
    dtype, down = {"e4m3": (ml_dtypes.float8_e4m3fn, 7), "e5m2": (ml_dtypes.float8_e5m2, 14)}[fmt]
    v = np.moveaxis(np.asarray(x, np.float32).astype(ml_dtypes.bfloat16).astype(np.float64), axis, -1)
    blocks = v.reshape(v.shape[:-1] + (-1, 32))
    amax = np.abs(blocks).max(-1, keepdims=True)
    byte = np.maximum(np.where(amax > 0, np.frexp(amax)[1] - 1 + 127, 0) - down, 1)
    scale = np.exp2(byte - 127.0)
    codes = (blocks / scale).astype(np.float32).astype(dtype).astype(np.float64)
    return np.moveaxis((codes * scale).reshape(v.shape), -1, axis)


WIDE = False


def mx_kscale(k):
    if not WIDE:
        return np.ones(k)
    levels = np.array([10, -10, 5, -5, 0])
    a = np.random.permutation(np.resize(levels, k // 512 * 4)).reshape(k // 512, 4)
    idx = np.arange(k)
    return np.exp2(a[idx // 512, idx % 128 // 32])


BF16 = ml_dtypes.bfloat16


def bf(x):
    return np.asarray(x, np.float32).astype(BF16)


def f64(x):
    return np.asarray(x).astype(np.float64)


E2M1 = np.array([0.0, 0.5, 1.0, 1.5, 2.0, 3.0, 4.0, 6.0, -0.0, -0.5, -1.0, -1.5, -2.0, -3.0, -4.0, -6.0])


def pack_weight(w, fmt):
    k, n = w.shape
    w = f64(bf(w)).reshape(k // 32, 32, n)
    amax = np.abs(w).max(1)
    if fmt == "e4m3":
        byte = np.frexp(amax)[1] - 1 + 127 - 7
    else:
        mant, ex = np.frexp(amax / 6.0)
        byte = np.where(mant > 0.5, ex, ex - 1) + 127
    byte = np.clip(np.where(amax > 0, byte, 1), 1, 254)
    scaled = (w * np.exp2(127.0 - byte)[:, None, :]).reshape(k, n).astype(np.float32)
    by_word = np.ascontiguousarray(scaled.reshape(k // 512, 128, 4, n).transpose(0, 1, 3, 2))
    if fmt == "e4m3":
        words = by_word.astype(ml_dtypes.float8_e4m3fn).view(np.uint8)
    else:
        c = by_word.astype(ml_dtypes.float4_e2m1fn).view(np.uint8) & 0xF
        words = c[..., 0::2] | (c[..., 1::2] << 4)
    return np.ascontiguousarray(words), np.ascontiguousarray(byte.astype(np.uint8).reshape(k // 512, 16, n))


def unpack_weight(words, scales, fmt):
    g, p, n, _ = words.shape
    if fmt == "e4m3":
        vals = np.ascontiguousarray(words).view(ml_dtypes.float8_e4m3fn).astype(np.float64)
    else:
        nib = np.empty((g, p, n, 4), np.uint8)
        nib[..., 0::2] = words & 0xF
        nib[..., 1::2] = words >> 4
        vals = E2M1[nib]
    vals = vals * np.repeat(np.exp2(scales.astype(np.float64) - 127.0), 8, axis=1)[..., None]
    return vals.transpose(0, 1, 3, 2).reshape(g * 512, n)


N, S, I, L, M = 128, 8, 512, 512, 256
D = I + L


def sigmoid(v):
    return 1.0 / (1.0 + np.exp(-v))


def setup_inputs():
    s = mx_kscale(D)
    r = np.random.standard_normal
    modulation = bf((r((N, S, I)) * s[:I]).reshape(N, S * I))
    h0 = bf((r((N, S, L)) * s[I:]).reshape(N, S * L))
    c_new = bf(0.75 * r((N, S * L)))
    Wo = r((S, L, D)) / np.sqrt(D) / s
    b_o = bf(0.3 * r((S, L)))
    Wy = r((S, M, L)) * 2.0 / np.sqrt(L)
    b_y = bf(0.2 * r((S, M)))
    Wo_words, Wo_scales = pack_weight(np.ascontiguousarray(Wo.swapaxes(1, 2)).reshape(-1, L), "e4m3")
    Wy_words, Wy_scales = pack_weight(np.ascontiguousarray(Wy.swapaxes(1, 2)).reshape(-1, M), "e4m3")
    return {"modulation": modulation,
            "h0": h0,
            "c_new": c_new,
            "Wo_words": Wo_words, "Wo_scales": Wo_scales, "b_o": b_o,
            "Wy_words": Wy_words, "Wy_scales": Wy_scales, "b_y": b_y}


def proj(aq, Wt, b):
    return (aq.transpose(1, 0, 2) @ Wt).transpose(1, 0, 2) + f64(b)


def reference(modulation, h0, c_new, Wo_words, Wo_scales, b_o, Wy_words, Wy_scales, b_y):
    x = f64(modulation).reshape(N, S, I)
    h = f64(h0).reshape(N, S, L)
    c = f64(c_new).reshape(N, S, L)
    xq = mxq(np.concatenate([x, h], axis=-1), 2, "e4m3")
    o = sigmoid(proj(xq, unpack_weight(Wo_words, Wo_scales, "e4m3").reshape(S, D, L), b_o))
    h_new = o * np.tanh(c)
    y = proj(mxq(h_new, 2, "e4m3"), unpack_weight(Wy_words, Wy_scales, "e4m3").reshape(S, L, M), b_y)
    return y.reshape(N, S * M)

@@ -1,0 +1,246 @@
+from contextlib import ExitStack
+
+import concourse.mybir as mybir
+from concourse.masks import make_identity
+
+F32 = mybir.dt.float32
+BF16 = mybir.dt.bfloat16
+I32 = mybir.dt.int32
+U32 = mybir.dt.uint32
+U8 = mybir.dt.uint8
+FP8X4 = mybir.dt.float8_e4m3fn_x4
+ACT = mybir.ActivationFunctionType
+
+P = 128
+STREAMS = 8
+FEAT = 512
+OUT = 256
+PACK = 4
+HALVES = 2
+WORDS = FEAT // 2
+PAIR = 2
+PLANES = 4
+QUADS = 4
+
+FLOPS = 2 * P * STREAMS * (HALVES * FEAT * FEAT + FEAT * OUT)
+
+
+def tile_flatlstm_pb_e_kernel(
+    tc, modulation, h0, c_new, Wo_words, Wo_scales, b_o, Wy_words, Wy_scales, b_y, out
+):
+    nc = tc.nc
+    with ExitStack() as stack:
+        keep = stack.enter_context(tc.tile_pool(name="keep", bufs=1))
+        work = stack.enter_context(tc.tile_pool(name="work", bufs=2))
+        psum = stack.enter_context(tc.psum_pool(name="psum", bufs=2))
+        stack.enter_context(tc.manual_schedule())
+
+        x_sb = keep.tile([P, STREAMS * FEAT], BF16)
+        h_sb = keep.tile([P, STREAMS * FEAT], BF16)
+        c_sb = keep.tile([P, STREAMS * FEAT], BF16)
+        wo_words = keep.tile([P, STREAMS * HALVES, FEAT], U32, align_bytes=64)
+        wy_words = keep.tile([P, STREAMS, OUT], U32, align_bytes=64)
+        wo_planes = keep.tile([P, STREAMS * HALVES // PLANES, FEAT], U8, align_bytes=64)
+        wy_planes = keep.tile([P, STREAMS // PLANES, OUT], U8, align_bytes=64)
+        xh_codes = keep.tile([P, STREAMS, HALVES * P], U32, align_bytes=64)
+        xh_scales = keep.tile([P, STREAMS, HALVES * P], U8, align_bytes=64)
+        hn_codes = keep.tile([P, STREAMS, P], U32, align_bytes=64)
+        hn_scales = keep.tile([P, STREAMS, P], U8, align_bytes=64)
+        tanh_c = keep.tile([P, STREAMS, P, PACK], F32)
+        y_sb = keep.tile([P, STREAMS, OUT], F32)
+        ident = keep.tile([P, P], F32)
+        ones = keep.tile([P, P], BF16)
+        bo_rows = keep.tile([P, FEAT], BF16)
+        bo_col = keep.tile([P, PACK, STREAMS], F32)
+        by_row = keep.tile([P, STREAMS * OUT], BF16)
+        by_all = keep.tile([P, STREAMS, OUT], BF16)
+        warm = keep.tile([P, 1], F32)
+
+        nc.vector.memset(wo_planes[:].rearrange("p a n -> p (a n)").bitcast(I32), 0)
+        nc.vector.memset(wy_planes[:].rearrange("p a n -> p (a n)").bitcast(I32), 0)
+        nc.vector.memset(warm[:], 0.0)
+        nc.vector.memset(bo_rows[:].bitcast(I32), 0)
+        nc.vector.memset(by_row[:].bitcast(I32), 0)
+        nc.vector.memset(ones[:], 1.0)
+        make_identity(nc, ident[:])
+
+        wo_dram = Wo_words.rearrange("g p n t -> g p (n t)").bitcast(I32)
+        wy_dram = Wy_words.rearrange("g p n t -> g p (n t)").bitcast(I32)
+        wo_scale_dram = Wo_scales.bitcast(I32)
+        wy_scale_dram = Wy_scales.bitcast(I32)
+
+        def load_planes(planes, scale_dram, block):
+            for quad in range(QUADS):
+                nc.sync.dma_start(
+                    out=planes[32 * quad : 32 * quad + 16, block, :].bitcast(I32),
+                    in_=scale_dram[PLANES * block : PLANES * (block + 1), 4 * quad : 4 * quad + 4, :],
+                )
+
+        def load_wo(s):
+            passes = slice(HALVES * s, HALVES * (s + 1))
+            nc.sync.dma_start(
+                out=wo_words[:, passes, :].bitcast(I32),
+                in_=wo_dram[passes].rearrange("g p w -> p g w"),
+            )
+
+        nc.scalar.dma_start(out=bo_rows[0:STREAMS, :], in_=b_o)
+        nc.scalar.dma_start(out=by_row[0:1, :], in_=b_y.rearrange("(o s) m -> o (s m)", o=1))
+        nc.scalar.activation(out=warm[:], in_=warm[:], func=ACT.Sigmoid)
+        for pair in range(STREAMS // PAIR):
+            cols = slice(PAIR * FEAT * pair, PAIR * FEAT * (pair + 1))
+            nc.sync.dma_start(out=c_sb[:, cols], in_=c_new[:, cols])
+            nc.sync.dma_start(out=x_sb[:, cols], in_=modulation[:, cols])
+            nc.sync.dma_start(out=h_sb[:, cols], in_=h0[:, cols])
+            load_planes(wo_planes, wo_scale_dram, pair)
+            load_wo(PAIR * pair)
+            load_wo(PAIR * pair + 1)
+        for block in range(STREAMS // PLANES):
+            load_planes(wy_planes, wy_scale_dram, block)
+        for pair in range(STREAMS // PAIR):
+            streams = slice(PAIR * pair, PAIR * (pair + 1))
+            nc.sync.dma_start(
+                out=wy_words[:, streams, :].bitcast(I32),
+                in_=wy_dram[streams].rearrange("g p w -> p g w"),
+            )
+
+        def transpose_words(dst, src_sb, s):
+            words = src_sb[:].bitcast(F32)
+            for u in range(HALVES):
+                nc.tensor.transpose(
+                    dst[:, u, :], words[:, WORDS * s + u : WORDS * (s + 1) : HALVES], ident[:]
+                )
+
+        def turn_c(s):
+            c_t = psum.tile([P, HALVES, P], F32, tag="c_t")
+            transpose_words(c_t, c_sb, s)
+            return c_t
+
+        def tanh_of_c(s, c_t):
+            nc.scalar.activation(
+                out=tanh_c[:, s].rearrange("p r (u e) -> p r u e", e=2),
+                in_=c_t[:].bitcast(BF16).rearrange("p u (r e) -> p r u e", e=2),
+                func=ACT.Tanh,
+            )
+
+        def turn_xh(s):
+            xh_t = psum.tile([P, HALVES, HALVES, P], F32, tag="xh_t")
+            transpose_words(xh_t[:, 0], x_sb, s)
+            transpose_words(xh_t[:, 1], h_sb, s)
+            xh_grouped = work.tile([P, HALVES * P * PACK], BF16, align_bytes=64)
+            nc.vector.tensor_copy(
+                out=xh_grouped[:].bitcast(F32).rearrange("p (g r u) -> p g r u", g=HALVES, u=HALVES),
+                in_=xh_t[:].rearrange("p g u r -> p g r u"),
+            )
+            return xh_grouped
+
+        def quantise_xh(s, xh_grouped):
+            nc.vector.quantize_mx(
+                out=xh_codes[:, s, :].bitcast(FP8X4), scales=xh_scales[:, s, :], in_=xh_grouped[:]
+            )
+
+        def first_product(s):
+            acc = psum.tile([P, FEAT], F32, tag="acc1")
+            for half in range(HALVES):
+                g = HALVES * s + half
+                rows = slice(P * half, P * (half + 1))
+                nc.tensor.matmul_mx(
+                    out=acc[:],
+                    lhsT=xh_codes[:, s, rows].bitcast(FP8X4),
+                    lhsT_scale=xh_scales[:, s, rows],
+                    rhs=wo_words[:, g, :].bitcast(FP8X4),
+                    rhs_scale=wo_planes[4 * (g % PLANES) : P, g // PLANES, :],
+                    start=(half == 0),
+                    stop=(half == HALVES - 1),
+                )
+            return acc
+
+        def leave_psum(acc):
+            pre = work.tile([P, PACK, P], F32)
+            nc.scalar.copy(out=pre[:], in_=acc[:].rearrange("r (p t) -> r t p", t=PACK))
+            return pre
+
+        def output_gate(s, pre):
+            pre_t = psum.tile([P, PACK, P], F32, tag="pre_t")
+            for t in range(PACK):
+                nc.tensor.transpose(pre_t[:, t, :], pre[:, t, :], ident[:])
+            o_t = work.tile([P, PACK, P], F32)
+            for t in range(PACK):
+                nc.scalar.activation(
+                    out=o_t[:, t, :], in_=pre_t[:, t, :], func=ACT.Sigmoid, bias=bo_col[:, t, s : s + 1]
+                )
+            return o_t
+
+        def gating_product(s, o_t):
+            hn_grouped = work.tile([P, P, PACK], BF16, align_bytes=64)
+            nc.vector.tensor_mul(
+                out=hn_grouped[:], in0=o_t[:].rearrange("p t r -> p r t"), in1=tanh_c[:, s]
+            )
+            return hn_grouped
+
+        def quantise_hn(s, hn_grouped):
+            nc.vector.quantize_mx(
+                out=hn_codes[:, s, :].bitcast(FP8X4),
+                scales=hn_scales[:, s, :],
+                in_=hn_grouped[:].rearrange("p r t -> p (r t)"),
+            )
+
+        def second_product(s):
+            acc = psum.tile([P, OUT], F32, tag="xh_t")
+            nc.tensor.matmul_mx(
+                out=acc[:],
+                lhsT=hn_codes[:, s, :].bitcast(FP8X4),
+                lhsT_scale=hn_scales[:, s, :],
+                rhs=wy_words[:, s, :].bitcast(FP8X4),
+                rhs_scale=wy_planes[4 * (s % PLANES) : P, s // PLANES, :],
+                start=True,
+                stop=True,
+            )
+            nc.vector.tensor_add(out=y_sb[:, s, :], in0=acc[:], in1=by_all[:, s, :])
+            nc.sync.dma_start(out=out[:, OUT * s : OUT * (s + 1)], in_=y_sb[:, s, :])
+
+        bo_t = psum.tile([P, HALVES, P], F32, tag="c_t")
+        transpose_words(bo_t, bo_rows, 0)
+        nc.vector.tensor_copy(
+            out=bo_col[:].rearrange("p (u e) s -> p u e s", e=2),
+            in_=bo_t[:].bitcast(BF16).rearrange("p u (s e) -> p u e s", e=2)[:, :, :, 0:STREAMS],
+        )
+
+        turned_c = {}
+        acc_of = {}
+        gate_of = {}
+        for i in range(-2, STREAMS + 2):
+            if 0 <= i - 1 < STREAMS:
+                pre = leave_psum(acc_of[i - 1])
+            if 0 <= i + 1 < STREAMS:
+                tanh_of_c(i + 1, turned_c[i + 1])
+            if 0 <= i - 2:
+                hn_grouped = gating_product(i - 2, gate_of[i - 2])
+            if 0 <= i + 1 < STREAMS:
+                xh_grouped = turn_xh(i + 1)
+            if 0 <= i - 1 < STREAMS:
+                gate_of[i - 1] = output_gate(i - 1, pre)
+            if i + 2 < STREAMS:
+                turned_c[i + 2] = turn_c(i + 2)
+            if 0 <= i - 2:
+                quantise_hn(i - 2, hn_grouped)
+            if 0 <= i + 1 < STREAMS:
+                quantise_xh(i + 1, xh_grouped)
+            if 0 <= i < STREAMS:
+                acc_of[i] = first_product(i)
+
+        by_flat = by_all[:].rearrange("p s m -> p (s m)")
+        for bank in range(2):
+            by_ps = psum.tile([P, 2 * FEAT], BF16, tag="acc1")
+            for part in range(2):
+                cols = slice(FEAT * (2 * bank + part), FEAT * (2 * bank + part + 1))
+                nc.tensor.matmul(
+                    out=by_ps[:, FEAT * part : FEAT * (part + 1)],
+                    lhsT=ones[:],
+                    rhs=by_row[:, cols],
+                    start=True,
+                    stop=True,
+                )
+            nc.scalar.copy(out=by_flat[:, 2 * FEAT * bank : 2 * FEAT * (bank + 1)], in_=by_ps[:])
+
+        for s in range(STREAMS):
+            second_product(s)

@@ -49,10 +49,8 @@ def tile_flatlstm_pb_e_kernel(
         tanh_c = keep.tile([P, STREAMS, P, PACK], F32)
         y_sb = keep.tile([P, STREAMS, OUT], F32)
         ident = keep.tile([P, P], F32)
-        ones = keep.tile([P, P], BF16)
         bo_rows = keep.tile([P, FEAT], BF16)
         bo_col = keep.tile([P, PACK, STREAMS], F32)
-        by_row = keep.tile([P, STREAMS * OUT], BF16)
         by_all = keep.tile([P, STREAMS, OUT], BF16)
         warm = keep.tile([P, 1], F32)
 
@@ -60,8 +58,6 @@ def tile_flatlstm_pb_e_kernel(
         nc.vector.memset(wy_planes[:].rearrange("p a n -> p (a n)").bitcast(I32), 0)
         nc.vector.memset(warm[:], 0.0)
         nc.vector.memset(bo_rows[:].bitcast(I32), 0)
-        nc.vector.memset(by_row[:].bitcast(I32), 0)
-        nc.vector.memset(ones[:], 1.0)
         make_identity(nc, ident[:])
 
         wo_dram = Wo_words.rearrange("g p n t -> g p (n t)").bitcast(I32)
@@ -84,16 +80,24 @@ def tile_flatlstm_pb_e_kernel(
             )
 
         nc.scalar.dma_start(out=bo_rows[0:STREAMS, :], in_=b_o)
-        nc.scalar.dma_start(out=by_row[0:1, :], in_=b_y.rearrange("(o s) m -> o (s m)", o=1))
         nc.scalar.activation(out=warm[:], in_=warm[:], func=ACT.Sigmoid)
-        for pair in range(STREAMS // PAIR):
+        def load_inputs(pair):
             cols = slice(PAIR * FEAT * pair, PAIR * FEAT * (pair + 1))
-            nc.sync.dma_start(out=c_sb[:, cols], in_=c_new[:, cols])
             nc.sync.dma_start(out=x_sb[:, cols], in_=modulation[:, cols])
             nc.sync.dma_start(out=h_sb[:, cols], in_=h0[:, cols])
+            nc.sync.dma_start(out=c_sb[:, cols], in_=c_new[:, cols])
+
+        load_inputs(0)
+        for pair in range(STREAMS // PAIR):
             load_planes(wo_planes, wo_scale_dram, pair)
             load_wo(PAIR * pair)
+            if pair + 1 < STREAMS // PAIR:
+                load_inputs(pair + 1)
             load_wo(PAIR * pair + 1)
+        nc.sync.dma_start(
+            out=by_all[:].rearrange("p s m -> p (s m)"),
+            in_=b_y.rearrange("s m -> (s m)").partition_broadcast(P),
+        )
         for block in range(STREAMS // PLANES):
             load_planes(wy_planes, wy_scale_dram, block)
         for pair in range(STREAMS // PAIR):
@@ -159,10 +163,13 @@ def tile_flatlstm_pb_e_kernel(
             nc.scalar.copy(out=pre[:], in_=acc[:].rearrange("r (p t) -> r t p", t=PACK))
             return pre
 
-        def output_gate(s, pre):
+        def turn_pre(pre):
             pre_t = psum.tile([P, PACK, P], F32, tag="pre_t")
             for t in range(PACK):
                 nc.tensor.transpose(pre_t[:, t, :], pre[:, t, :], ident[:])
+            return pre_t
+
+        def output_gate(s, pre_t):
             o_t = work.tile([P, PACK, P], F32)
             for t in range(PACK):
                 nc.scalar.activation(
@@ -184,19 +191,28 @@ def tile_flatlstm_pb_e_kernel(
                 in_=hn_grouped[:].rearrange("p r t -> p (r t)"),
             )
 
-        def second_product(s):
-            acc = psum.tile([P, OUT], F32, tag="xh_t")
-            nc.tensor.matmul_mx(
-                out=acc[:],
-                lhsT=hn_codes[:, s, :].bitcast(FP8X4),
-                lhsT_scale=hn_scales[:, s, :],
-                rhs=wy_words[:, s, :].bitcast(FP8X4),
-                rhs_scale=wy_planes[4 * (s % PLANES) : P, s // PLANES, :],
-                start=True,
-                stop=True,
+        def second_product(pair):
+            acc = psum.tile([P, PAIR, OUT], F32, tag="xh_t")
+            for j in range(PAIR):
+                s = PAIR * pair + j
+                nc.tensor.matmul_mx(
+                    out=acc[:, j, :],
+                    lhsT=hn_codes[:, s, :].bitcast(FP8X4),
+                    lhsT_scale=hn_scales[:, s, :],
+                    rhs=wy_words[:, s, :].bitcast(FP8X4),
+                    rhs_scale=wy_planes[4 * (s % PLANES) : P, s // PLANES, :],
+                    start=True,
+                    stop=True,
+                )
+            return acc
+
+        def finish(pair, acc):
+            streams = slice(PAIR * pair, PAIR * (pair + 1))
+            nc.vector.tensor_add(out=y_sb[:, streams, :], in0=acc[:], in1=by_all[:, streams, :])
+            nc.sync.dma_start(
+                out=out[:, PAIR * OUT * pair : PAIR * OUT * (pair + 1)],
+                in_=y_sb[:, streams, :].rearrange("p s m -> p (s m)"),
             )
-            nc.vector.tensor_add(out=y_sb[:, s, :], in0=acc[:], in1=by_all[:, s, :])
-            nc.sync.dma_start(out=out[:, OUT * s : OUT * (s + 1)], in_=y_sb[:, s, :])
 
         bo_t = psum.tile([P, HALVES, P], F32, tag="c_t")
         transpose_words(bo_t, bo_rows, 0)
@@ -205,42 +221,28 @@ def tile_flatlstm_pb_e_kernel(
             in_=bo_t[:].bitcast(BF16).rearrange("p u (s e) -> p u e s", e=2)[:, :, :, 0:STREAMS],
         )
 
-        turned_c = {}
         acc_of = {}
+        turned_pre = {}
         gate_of = {}
-        for i in range(-2, STREAMS + 2):
+        for i in range(-1, STREAMS + STREAMS // PAIR):
+            if i >= STREAMS:
+                y_acc = second_product(i - STREAMS)
             if 0 <= i - 1 < STREAMS:
                 pre = leave_psum(acc_of[i - 1])
-            if 0 <= i + 1 < STREAMS:
-                tanh_of_c(i + 1, turned_c[i + 1])
-            if 0 <= i - 2:
-                hn_grouped = gating_product(i - 2, gate_of[i - 2])
-            if 0 <= i + 1 < STREAMS:
+            if 0 <= i - 2 < STREAMS:
+                gate_of[i - 2] = output_gate(i - 2, turned_pre[i - 2])
+            if 0 <= i - 3 < STREAMS:
+                hn_grouped = gating_product(i - 3, gate_of[i - 3])
+            if i + 1 < STREAMS:
                 xh_grouped = turn_xh(i + 1)
+                tanh_of_c(i + 1, turn_c(i + 1))
             if 0 <= i - 1 < STREAMS:
-                gate_of[i - 1] = output_gate(i - 1, pre)
-            if i + 2 < STREAMS:
-                turned_c[i + 2] = turn_c(i + 2)
-            if 0 <= i - 2:
-                quantise_hn(i - 2, hn_grouped)
-            if 0 <= i + 1 < STREAMS:
+                turned_pre[i - 1] = turn_pre(pre)
+            if 0 <= i - 3 < STREAMS:
+                quantise_hn(i - 3, hn_grouped)
+            if i + 1 < STREAMS:
                 quantise_xh(i + 1, xh_grouped)
             if 0 <= i < STREAMS:
                 acc_of[i] = first_product(i)
-
-        by_flat = by_all[:].rearrange("p s m -> p (s m)")
-        for bank in range(2):
-            by_ps = psum.tile([P, 2 * FEAT], BF16, tag="acc1")
-            for part in range(2):
-                cols = slice(FEAT * (2 * bank + part), FEAT * (2 * bank + part + 1))
-                nc.tensor.matmul(
-                    out=by_ps[:, FEAT * part : FEAT * (part + 1)],
-                    lhsT=ones[:],
-                    rhs=by_row[:, cols],
-                    start=True,
-                    stop=True,
-                )
-            nc.scalar.copy(out=by_flat[:, 2 * FEAT * bank : 2 * FEAT * (bank + 1)], in_=by_ps[:])
-
-        for s in range(STREAMS):
-            second_product(s)
+            if i >= STREAMS:
+                finish(i - STREAMS, y_acc)

@@ -49,6 +49,8 @@ def tile_flatlstm_pb_e_kernel(
         tanh_c = keep.tile([P, STREAMS, P, PACK], F32)
         y_sb = keep.tile([P, STREAMS, OUT], F32)
         ident = keep.tile([P, P], F32)
+        ones = keep.tile([P, P], BF16)
+        by_row = keep.tile([P, STREAMS * OUT], BF16)
         bo_rows = keep.tile([P, FEAT], BF16)
         bo_col = keep.tile([P, PACK, STREAMS], F32)
         by_all = keep.tile([P, STREAMS, OUT], BF16)
@@ -58,6 +60,8 @@ def tile_flatlstm_pb_e_kernel(
         nc.vector.memset(wy_planes[:].rearrange("p a n -> p (a n)").bitcast(I32), 0)
         nc.vector.memset(warm[:], 0.0)
         nc.vector.memset(bo_rows[:].bitcast(I32), 0)
+        nc.vector.memset(by_row[:].bitcast(I32), 0)
+        nc.vector.memset(ones[:], 1.0)
         make_identity(nc, ident[:])
 
         wo_dram = Wo_words.rearrange("g p n t -> g p (n t)").bitcast(I32)
@@ -80,6 +84,7 @@ def tile_flatlstm_pb_e_kernel(
             )
 
         nc.scalar.dma_start(out=bo_rows[0:STREAMS, :], in_=b_o)
+        nc.scalar.dma_start(out=by_row[0:1, :], in_=b_y.rearrange("(o s) m -> o (s m)", o=1))
         nc.scalar.activation(out=warm[:], in_=warm[:], func=ACT.Sigmoid)
         def load_inputs(pair):
             cols = slice(PAIR * FEAT * pair, PAIR * FEAT * (pair + 1))
@@ -94,10 +99,6 @@ def tile_flatlstm_pb_e_kernel(
             if pair + 1 < STREAMS // PAIR:
                 load_inputs(pair + 1)
             load_wo(PAIR * pair + 1)
-        nc.sync.dma_start(
-            out=by_all[:].rearrange("p s m -> p (s m)"),
-            in_=b_y.rearrange("s m -> (s m)").partition_broadcast(P),
-        )
         for block in range(STREAMS // PLANES):
             load_planes(wy_planes, wy_scale_dram, block)
         for pair in range(STREAMS // PAIR):
@@ -191,6 +192,21 @@ def tile_flatlstm_pb_e_kernel(
                 in_=hn_grouped[:].rearrange("p r t -> p (r t)"),
             )
 
+        def spread_by():
+            by_flat = by_all[:].rearrange("p s m -> p (s m)")
+            for bank in range(2):
+                by_ps = psum.tile([P, 2 * FEAT], BF16, tag="xh_t")
+                for part in range(2):
+                    cols = slice(FEAT * (2 * bank + part), FEAT * (2 * bank + part + 1))
+                    nc.tensor.matmul(
+                        out=by_ps[:, FEAT * part : FEAT * (part + 1)],
+                        lhsT=ones[:],
+                        rhs=by_row[:, cols],
+                        start=True,
+                        stop=True,
+                    )
+                nc.scalar.copy(out=by_flat[:, 2 * FEAT * bank : 2 * FEAT * (bank + 1)], in_=by_ps[:])
+
         def second_product(pair):
             acc = psum.tile([P, PAIR, OUT], F32, tag="xh_t")
             for j in range(PAIR):
@@ -236,6 +252,8 @@ def tile_flatlstm_pb_e_kernel(
             if i + 1 < STREAMS:
                 xh_grouped = turn_xh(i + 1)
                 tanh_of_c(i + 1, turn_c(i + 1))
+            if i + 1 == STREAMS:
+                spread_by()
             if 0 <= i - 1 < STREAMS:
                 turned_pre[i - 1] = turn_pre(pre)
             if 0 <= i - 3 < STREAMS:

@@ -205,7 +205,7 @@ def tile_flatlstm_pb_e_kernel(
                         start=True,
                         stop=True,
                     )
-                nc.scalar.copy(out=by_flat[:, 2 * FEAT * bank : 2 * FEAT * (bank + 1)], in_=by_ps[:])
+                nc.vector.tensor_copy(out=by_flat[:, 2 * FEAT * bank : 2 * FEAT * (bank + 1)], in_=by_ps[:])
 
         def second_product(pair):
             acc = psum.tile([P, PAIR, OUT], F32, tag="xh_t")
@@ -238,29 +238,30 @@ def tile_flatlstm_pb_e_kernel(
         )
 
         acc_of = {}
+        sorted_pre = {}
         turned_pre = {}
         gate_of = {}
-        for i in range(-1, STREAMS + STREAMS // PAIR):
-            if i >= STREAMS:
-                y_acc = second_product(i - STREAMS)
+        for i in range(-1, STREAMS + 1 + STREAMS // PAIR):
+            if i > STREAMS:
+                y_acc = second_product(i - STREAMS - 1)
             if 0 <= i - 1 < STREAMS:
-                pre = leave_psum(acc_of[i - 1])
-            if 0 <= i - 2 < STREAMS:
-                gate_of[i - 2] = output_gate(i - 2, turned_pre[i - 2])
+                sorted_pre[i - 1] = leave_psum(acc_of[i - 1])
             if 0 <= i - 3 < STREAMS:
-                hn_grouped = gating_product(i - 3, gate_of[i - 3])
+                gate_of[i - 3] = output_gate(i - 3, turned_pre[i - 3])
+            if 0 <= i - 4 < STREAMS:
+                hn_grouped = gating_product(i - 4, gate_of[i - 4])
+            if 0 <= i - 2 < STREAMS:
+                turned_pre[i - 2] = turn_pre(sorted_pre[i - 2])
             if i + 1 < STREAMS:
                 xh_grouped = turn_xh(i + 1)
                 tanh_of_c(i + 1, turn_c(i + 1))
             if i + 1 == STREAMS:
                 spread_by()
-            if 0 <= i - 1 < STREAMS:
-                turned_pre[i - 1] = turn_pre(pre)
-            if 0 <= i - 3 < STREAMS:
-                quantise_hn(i - 3, hn_grouped)
+            if 0 <= i - 4 < STREAMS:
+                quantise_hn(i - 4, hn_grouped)
             if i + 1 < STREAMS:
                 quantise_xh(i + 1, xh_grouped)
             if 0 <= i < STREAMS:
                 acc_of[i] = first_product(i)
-            if i >= STREAMS:
-                finish(i - STREAMS, y_acc)
+            if i > STREAMS:
+                finish(i - STREAMS - 1, y_acc)

@@ -238,30 +238,29 @@ def tile_flatlstm_pb_e_kernel(
         )
 
         acc_of = {}
-        sorted_pre = {}
         turned_pre = {}
         gate_of = {}
-        for i in range(-1, STREAMS + 1 + STREAMS // PAIR):
-            if i > STREAMS:
-                y_acc = second_product(i - STREAMS - 1)
+        for i in range(-1, STREAMS + STREAMS // PAIR):
+            if i >= STREAMS:
+                y_acc = second_product(i - STREAMS)
             if 0 <= i - 1 < STREAMS:
-                sorted_pre[i - 1] = leave_psum(acc_of[i - 1])
-            if 0 <= i - 3 < STREAMS:
-                gate_of[i - 3] = output_gate(i - 3, turned_pre[i - 3])
-            if 0 <= i - 4 < STREAMS:
-                hn_grouped = gating_product(i - 4, gate_of[i - 4])
+                pre = leave_psum(acc_of[i - 1])
             if 0 <= i - 2 < STREAMS:
-                turned_pre[i - 2] = turn_pre(sorted_pre[i - 2])
+                gate_of[i - 2] = output_gate(i - 2, turned_pre[i - 2])
+            if 0 <= i - 3 < STREAMS:
+                hn_grouped = gating_product(i - 3, gate_of[i - 3])
             if i + 1 < STREAMS:
                 xh_grouped = turn_xh(i + 1)
                 tanh_of_c(i + 1, turn_c(i + 1))
             if i + 1 == STREAMS:
                 spread_by()
-            if 0 <= i - 4 < STREAMS:
-                quantise_hn(i - 4, hn_grouped)
+            if 0 <= i - 1 < STREAMS:
+                turned_pre[i - 1] = turn_pre(pre)
+            if 0 <= i - 3 < STREAMS:
+                quantise_hn(i - 3, hn_grouped)
             if i + 1 < STREAMS:
                 quantise_xh(i + 1, xh_grouped)
             if 0 <= i < STREAMS:
                 acc_of[i] = first_product(i)
-            if i > STREAMS:
-                finish(i - STREAMS - 1, y_acc)
+            if i >= STREAMS:
+                finish(i - STREAMS, y_acc)

@@ -254,13 +254,13 @@ def tile_flatlstm_pb_e_kernel(
                 tanh_of_c(i + 1, turn_c(i + 1))
             if i + 1 == STREAMS:
                 spread_by()
+            if 0 <= i < STREAMS:
+                acc_of[i] = first_product(i)
             if 0 <= i - 1 < STREAMS:
                 turned_pre[i - 1] = turn_pre(pre)
             if 0 <= i - 3 < STREAMS:
                 quantise_hn(i - 3, hn_grouped)
             if i + 1 < STREAMS:
                 quantise_xh(i + 1, xh_grouped)
-            if 0 <= i < STREAMS:
-                acc_of[i] = first_product(i)
             if i >= STREAMS:
                 finish(i - STREAMS, y_acc)

@@ -41,7 +41,7 @@ def tile_flatlstm_pb_e_kernel(
         wo_words = keep.tile([P, STREAMS * HALVES, FEAT], U32, align_bytes=64)
         wy_words = keep.tile([P, STREAMS, OUT], U32, align_bytes=64)
         wo_planes = keep.tile([P, STREAMS * HALVES // PLANES, FEAT], U8, align_bytes=64)
-        wy_planes = keep.tile([P, STREAMS // PLANES, OUT], U8, align_bytes=64)
+        wy_planes = keep.tile([P, STREAMS, OUT], U8, align_bytes=64)
         xh_codes = keep.tile([P, STREAMS, HALVES * P], U32, align_bytes=64)
         xh_scales = keep.tile([P, STREAMS, HALVES * P], U8, align_bytes=64)
         hn_codes = keep.tile([P, STREAMS, P], U32, align_bytes=64)
@@ -83,24 +83,38 @@ def tile_flatlstm_pb_e_kernel(
                 in_=wo_dram[passes].rearrange("g p w -> p g w"),
             )
 
-        nc.scalar.dma_start(out=bo_rows[0:STREAMS, :], in_=b_o)
-        nc.scalar.dma_start(out=by_row[0:1, :], in_=b_y.rearrange("(o s) m -> o (s m)", o=1))
         nc.scalar.activation(out=warm[:], in_=warm[:], func=ACT.Sigmoid)
-        def load_inputs(pair):
+        def load_xh(pair):
             cols = slice(PAIR * FEAT * pair, PAIR * FEAT * (pair + 1))
             nc.sync.dma_start(out=x_sb[:, cols], in_=modulation[:, cols])
             nc.sync.dma_start(out=h_sb[:, cols], in_=h0[:, cols])
+
+        def load_c(pair):
+            cols = slice(PAIR * FEAT * pair, PAIR * FEAT * (pair + 1))
             nc.sync.dma_start(out=c_sb[:, cols], in_=c_new[:, cols])
 
-        load_inputs(0)
+        def load_inputs(pair):
+            load_xh(pair)
+            load_c(pair)
+
+        load_xh(0)
+        load_wo(0)
+        load_c(0)
+        load_planes(wo_planes, wo_scale_dram, 0)
+        nc.scalar.dma_start(out=bo_rows[0:STREAMS, :], in_=b_o)
+        nc.scalar.dma_start(out=by_row[0:1, :], in_=b_y.rearrange("(o s) m -> o (s m)", o=1))
         for pair in range(STREAMS // PAIR):
-            load_planes(wo_planes, wo_scale_dram, pair)
-            load_wo(PAIR * pair)
+            if pair > 0:
+                load_planes(wo_planes, wo_scale_dram, pair)
+                load_wo(PAIR * pair)
             if pair + 1 < STREAMS // PAIR:
                 load_inputs(pair + 1)
             load_wo(PAIR * pair + 1)
-        for block in range(STREAMS // PLANES):
-            load_planes(wy_planes, wy_scale_dram, block)
+        for quad in range(QUADS):
+            nc.sync.dma_start(
+                out=wy_planes[32 * quad : 32 * quad + 4, :, :].rearrange("r g n -> r (g n)").bitcast(I32).rearrange("r (g w) -> r g w", g=STREAMS),
+                in_=wy_scale_dram[:, 4 * quad : 4 * quad + 4, :].rearrange("g r w -> r g w"),
+            )
         for pair in range(STREAMS // PAIR):
             streams = slice(PAIR * pair, PAIR * (pair + 1))
             nc.sync.dma_start(
@@ -208,7 +222,7 @@ def tile_flatlstm_pb_e_kernel(
                 nc.vector.tensor_copy(out=by_flat[:, 2 * FEAT * bank : 2 * FEAT * (bank + 1)], in_=by_ps[:])
 
         def second_product(pair):
-            acc = psum.tile([P, PAIR, OUT], F32, tag="xh_t")
+            acc = psum.tile([P, PAIR, OUT], F32, tag=("xh_t" if pair < 2 else "c_t"))
             for j in range(PAIR):
                 s = PAIR * pair + j
                 nc.tensor.matmul_mx(
@@ -216,7 +230,7 @@ def tile_flatlstm_pb_e_kernel(
                     lhsT=hn_codes[:, s, :].bitcast(FP8X4),
                     lhsT_scale=hn_scales[:, s, :],
                     rhs=wy_words[:, s, :].bitcast(FP8X4),
-                    rhs_scale=wy_planes[4 * (s % PLANES) : P, s // PLANES, :],
+                    rhs_scale=wy_planes[:, s, :],
                     start=True,
                     stop=True,
                 )
@@ -230,37 +244,66 @@ def tile_flatlstm_pb_e_kernel(
                 in_=y_sb[:, streams, :].rearrange("p s m -> p (s m)"),
             )
 
-        bo_t = psum.tile([P, HALVES, P], F32, tag="c_t")
-        transpose_words(bo_t, bo_rows, 0)
-        nc.vector.tensor_copy(
-            out=bo_col[:].rearrange("p (u e) s -> p u e s", e=2),
-            in_=bo_t[:].bitcast(BF16).rearrange("p u (s e) -> p u e s", e=2)[:, :, :, 0:STREAMS],
-        )
+        def turn_bo():
+            bo_t = psum.tile([P, HALVES, P], F32, tag="c_t")
+            transpose_words(bo_t, bo_rows, 0)
+            nc.vector.tensor_copy(
+                out=bo_col[:].rearrange("p (u e) s -> p u e s", e=2),
+                in_=bo_t[:].bitcast(BF16).rearrange("p u (s e) -> p u e s", e=2)[:, :, :, 0:STREAMS],
+            )
 
-        acc_of = {}
-        turned_pre = {}
+        pre_of = {}
         gate_of = {}
-        for i in range(-1, STREAMS + STREAMS // PAIR):
-            if i >= STREAMS:
-                y_acc = second_product(i - STREAMS)
-            if 0 <= i - 1 < STREAMS:
-                pre = leave_psum(acc_of[i - 1])
-            if 0 <= i - 2 < STREAMS:
-                gate_of[i - 2] = output_gate(i - 2, turned_pre[i - 2])
-            if 0 <= i - 3 < STREAMS:
-                hn_grouped = gating_product(i - 3, gate_of[i - 3])
-            if i + 1 < STREAMS:
-                xh_grouped = turn_xh(i + 1)
-                tanh_of_c(i + 1, turn_c(i + 1))
-            if i + 1 == STREAMS:
+        xh_of = {}
+        hn_of = {}
+
+        def live(s):
+            return 0 <= s < STREAMS
+
+        def multiply(s):
+            pre_of[s] = leave_psum(first_product(s))
+
+        def gate(s):
+            gate_of[s] = output_gate(s, turn_pre(pre_of[s]))
+
+        for period in range(-1, STREAMS // PAIR + 1):
+            a = PAIR * period
+            b = a + 1
+            n0 = a + 2
+            n1 = a + 3
+            if live(a):
+                multiply(a)
+            if period == 0:
+                turn_bo()
+            if live(a - 1):
+                gate(a - 1)
+            if live(n0):
+                xh_of[n0] = turn_xh(n0)
+                xh_of[n1] = turn_xh(n1)
+            elif live(b):
+                multiply(b)
+            if live(a):
+                gate(a)
+            if a - 1 == STREAMS - 1:
+                finish(0, second_product(0))
+            if live(a - 1):
+                hn_of[a - 1] = gating_product(a - 1, gate_of[a - 1])
+            if live(n0):
+                c_t0 = turn_c(n0)
+                c_t1 = turn_c(n1)
+                tanh_of_c(n0, c_t0)
+                quantise_xh(n0, xh_of[n0])
+                quantise_xh(n1, xh_of[n1])
+            if live(a - 1):
+                quantise_hn(a - 1, hn_of[a - 1])
+            if period == 0:
                 spread_by()
-            if 0 <= i < STREAMS:
-                acc_of[i] = first_product(i)
-            if 0 <= i - 1 < STREAMS:
-                turned_pre[i - 1] = turn_pre(pre)
-            if 0 <= i - 3 < STREAMS:
-                quantise_hn(i - 3, hn_grouped)
-            if i + 1 < STREAMS:
-                quantise_xh(i + 1, xh_grouped)
-            if i >= STREAMS:
-                finish(i - STREAMS, y_acc)
+            if live(n0):
+                if live(b):
+                    multiply(b)
+                tanh_of_c(n1, c_t1)
+            if live(a):
+                hn_of[a] = gating_product(a, gate_of[a])
+                quantise_hn(a, hn_of[a])
+        for pair in range(1, STREAMS // PAIR):
+            finish(pair, second_product(pair))

@@ -266,7 +266,7 @@ def tile_flatlstm_pb_e_kernel(
         def gate(s):
             gate_of[s] = output_gate(s, turn_pre(pre_of[s]))
 
-        for period in range(-1, STREAMS // PAIR + 1):
+        for period in range(-1, STREAMS // PAIR - 1):
             a = PAIR * period
             b = a + 1
             n0 = a + 2
@@ -280,12 +280,8 @@ def tile_flatlstm_pb_e_kernel(
             if live(n0):
                 xh_of[n0] = turn_xh(n0)
                 xh_of[n1] = turn_xh(n1)
-            elif live(b):
-                multiply(b)
             if live(a):
                 gate(a)
-            if a - 1 == STREAMS - 1:
-                finish(0, second_product(0))
             if live(a - 1):
                 hn_of[a - 1] = gating_product(a - 1, gate_of[a - 1])
             if live(n0):
@@ -305,5 +301,17 @@ def tile_flatlstm_pb_e_kernel(
             if live(a):
                 hn_of[a] = gating_product(a, gate_of[a])
                 quantise_hn(a, hn_of[a])
+        multiply(6)
+        gate(5)
+        multiply(7)
+        gate(6)
+        hn_of[5] = gating_product(5, gate_of[5])
+        finish(0, second_product(0))
+        quantise_hn(5, hn_of[5])
+        hn_of[6] = gating_product(6, gate_of[6])
+        gate(7)
+        hn_of[7] = gating_product(7, gate_of[7])
+        quantise_hn(6, hn_of[6])
+        quantise_hn(7, hn_of[7])
         for pair in range(1, STREAMS // PAIR):
             finish(pair, second_product(pair))

@@ -109,7 +109,10 @@ def tile_flatlstm_pb_e_kernel(
                 load_wo(PAIR * pair)
             if pair + 1 < STREAMS // PAIR:
                 load_inputs(pair + 1)
-            load_wo(PAIR * pair + 1)
+            if pair + 1 < STREAMS // PAIR:
+                load_wo(PAIR * pair + 1)
+        for g in (HALVES * STREAMS - 2, HALVES * STREAMS - 1):
+            nc.sync.dma_start(out=wo_words[:, g, :].bitcast(I32), in_=wo_dram[g])
         for quad in range(QUADS):
             nc.sync.dma_start(
                 out=wy_planes[32 * quad : 32 * quad + 4, :, :].rearrange("r g n -> r (g n)").bitcast(I32).rearrange("r (g w) -> r g w", g=STREAMS),

from contextlib import ExitStack

import concourse.mybir as mybir
from concourse.masks import make_identity

F32 = mybir.dt.float32
BF16 = mybir.dt.bfloat16
I32 = mybir.dt.int32
U32 = mybir.dt.uint32
U8 = mybir.dt.uint8
FP8X4 = mybir.dt.float8_e4m3fn_x4
ACT = mybir.ActivationFunctionType

P = 128
STREAMS = 8
FEAT = 512
OUT = 256
PACK = 4
HALVES = 2
WORDS = FEAT // 2
PAIR = 2
PLANES = 4
QUADS = 4

FLOPS = 2 * P * STREAMS * (HALVES * FEAT * FEAT + FEAT * OUT)


def tile_flatlstm_pb_e_kernel(
    tc, modulation, h0, c_new, Wo_words, Wo_scales, b_o, Wy_words, Wy_scales, b_y, out
):
    nc = tc.nc
    with ExitStack() as stack:
        keep = stack.enter_context(tc.tile_pool(name="keep", bufs=1))
        work = stack.enter_context(tc.tile_pool(name="work", bufs=2))
        psum = stack.enter_context(tc.psum_pool(name="psum", bufs=2))
        stack.enter_context(tc.manual_schedule())

        x_sb = keep.tile([P, STREAMS * FEAT], BF16)
        h_sb = keep.tile([P, STREAMS * FEAT], BF16)
        c_sb = keep.tile([P, STREAMS * FEAT], BF16)
        wo_words = keep.tile([P, STREAMS * HALVES, FEAT], U32, align_bytes=64)
        wy_words = keep.tile([P, STREAMS, OUT], U32, align_bytes=64)
        wo_planes = keep.tile([P, STREAMS * HALVES // PLANES, FEAT], U8, align_bytes=64)
        wy_planes = keep.tile([P, STREAMS, OUT], U8, align_bytes=64)
        xh_codes = keep.tile([P, STREAMS, HALVES * P], U32, align_bytes=64)
        xh_scales = keep.tile([P, STREAMS, HALVES * P], U8, align_bytes=64)
        hn_codes = keep.tile([P, STREAMS, P], U32, align_bytes=64)
        hn_scales = keep.tile([P, STREAMS, P], U8, align_bytes=64)
        tanh_c = keep.tile([P, STREAMS, P, PACK], F32)
        y_sb = keep.tile([P, STREAMS, OUT], F32)
        ident = keep.tile([P, P], F32)
        ones = keep.tile([P, P], BF16)
        by_row = keep.tile([P, STREAMS * OUT], BF16)
        bo_rows = keep.tile([P, FEAT], BF16)
        bo_col = keep.tile([P, PACK, STREAMS], F32)
        by_all = keep.tile([P, STREAMS, OUT], BF16)
        warm = keep.tile([P, 1], F32)

        nc.vector.memset(wo_planes[:].rearrange("p a n -> p (a n)").bitcast(I32), 0)
        nc.vector.memset(wy_planes[:].rearrange("p a n -> p (a n)").bitcast(I32), 0)
        nc.vector.memset(warm[:], 0.0)
        nc.vector.memset(bo_rows[:].bitcast(I32), 0)
        nc.vector.memset(by_row[:].bitcast(I32), 0)
        nc.vector.memset(ones[:], 1.0)
        make_identity(nc, ident[:])

        wo_dram = Wo_words.rearrange("g p n t -> g p (n t)").bitcast(I32)
        wy_dram = Wy_words.rearrange("g p n t -> g p (n t)").bitcast(I32)
        wo_scale_dram = Wo_scales.bitcast(I32)
        wy_scale_dram = Wy_scales.bitcast(I32)

        def load_planes(planes, scale_dram, block):
            for quad in range(QUADS):
                nc.sync.dma_start(
                    out=planes[32 * quad : 32 * quad + 16, block, :].bitcast(I32),
                    in_=scale_dram[PLANES * block : PLANES * (block + 1), 4 * quad : 4 * quad + 4, :],
                )

        def load_wo(s):
            passes = slice(HALVES * s, HALVES * (s + 1))
            nc.sync.dma_start(
                out=wo_words[:, passes, :].bitcast(I32),
                in_=wo_dram[passes].rearrange("g p w -> p g w"),
            )

        nc.scalar.activation(out=warm[:], in_=warm[:], func=ACT.Sigmoid)
        def load_xh(pair):
            cols = slice(PAIR * FEAT * pair, PAIR * FEAT * (pair + 1))
            nc.sync.dma_start(out=x_sb[:, cols], in_=modulation[:, cols])
            nc.sync.dma_start(out=h_sb[:, cols], in_=h0[:, cols])

        def load_c(pair):
            cols = slice(PAIR * FEAT * pair, PAIR * FEAT * (pair + 1))
            nc.sync.dma_start(out=c_sb[:, cols], in_=c_new[:, cols])

        def load_inputs(pair):
            load_xh(pair)
            load_c(pair)

        load_xh(0)
        load_wo(0)
        load_c(0)
        load_planes(wo_planes, wo_scale_dram, 0)
        nc.scalar.dma_start(out=bo_rows[0:STREAMS, :], in_=b_o)
        nc.scalar.dma_start(out=by_row[0:1, :], in_=b_y.rearrange("(o s) m -> o (s m)", o=1))
        for pair in range(STREAMS // PAIR):
            if pair > 0:
                load_planes(wo_planes, wo_scale_dram, pair)
                load_wo(PAIR * pair)
            if pair + 1 < STREAMS // PAIR:
                load_inputs(pair + 1)
            if pair + 1 < STREAMS // PAIR:
                load_wo(PAIR * pair + 1)
        for g in (HALVES * STREAMS - 2, HALVES * STREAMS - 1):
            nc.sync.dma_start(out=wo_words[:, g, :].bitcast(I32), in_=wo_dram[g])
        for quad in range(QUADS):
            nc.sync.dma_start(
                out=wy_planes[32 * quad : 32 * quad + 4, :, :].rearrange("r g n -> r (g n)").bitcast(I32).rearrange("r (g w) -> r g w", g=STREAMS),
                in_=wy_scale_dram[:, 4 * quad : 4 * quad + 4, :].rearrange("g r w -> r g w"),
            )
        for pair in range(STREAMS // PAIR):
            streams = slice(PAIR * pair, PAIR * (pair + 1))
            nc.sync.dma_start(
                out=wy_words[:, streams, :].bitcast(I32),
                in_=wy_dram[streams].rearrange("g p w -> p g w"),
            )

        def transpose_words(dst, src_sb, s):
            words = src_sb[:].bitcast(F32)
            for u in range(HALVES):
                nc.tensor.transpose(
                    dst[:, u, :], words[:, WORDS * s + u : WORDS * (s + 1) : HALVES], ident[:]
                )

        def turn_c(s):
            c_t = psum.tile([P, HALVES, P], F32, tag="c_t")
            transpose_words(c_t, c_sb, s)
            return c_t

        def tanh_of_c(s, c_t):
            nc.scalar.activation(
                out=tanh_c[:, s].rearrange("p r (u e) -> p r u e", e=2),
                in_=c_t[:].bitcast(BF16).rearrange("p u (r e) -> p r u e", e=2),
                func=ACT.Tanh,
            )

        def turn_xh(s):
            xh_t = psum.tile([P, HALVES, HALVES, P], F32, tag="xh_t")
            transpose_words(xh_t[:, 0], x_sb, s)
            transpose_words(xh_t[:, 1], h_sb, s)
            xh_grouped = work.tile([P, HALVES * P * PACK], BF16, align_bytes=64)
            nc.vector.tensor_copy(
                out=xh_grouped[:].bitcast(F32).rearrange("p (g r u) -> p g r u", g=HALVES, u=HALVES),
                in_=xh_t[:].rearrange("p g u r -> p g r u"),
            )
            return xh_grouped

        def quantise_xh(s, xh_grouped):
            nc.vector.quantize_mx(
                out=xh_codes[:, s, :].bitcast(FP8X4), scales=xh_scales[:, s, :], in_=xh_grouped[:]
            )

        def first_product(s):
            acc = psum.tile([P, FEAT], F32, tag="acc1")
            for half in range(HALVES):
                g = HALVES * s + half
                rows = slice(P * half, P * (half + 1))
                nc.tensor.matmul_mx(
                    out=acc[:],
                    lhsT=xh_codes[:, s, rows].bitcast(FP8X4),
                    lhsT_scale=xh_scales[:, s, rows],
                    rhs=wo_words[:, g, :].bitcast(FP8X4),
                    rhs_scale=wo_planes[4 * (g % PLANES) : P, g // PLANES, :],
                    start=(half == 0),
                    stop=(half == HALVES - 1),
                )
            return acc

        def leave_psum(acc):
            pre = work.tile([P, PACK, P], F32)
            nc.scalar.copy(out=pre[:], in_=acc[:].rearrange("r (p t) -> r t p", t=PACK))
            return pre

        def turn_pre(pre):
            pre_t = psum.tile([P, PACK, P], F32, tag="pre_t")
            for t in range(PACK):
                nc.tensor.transpose(pre_t[:, t, :], pre[:, t, :], ident[:])
            return pre_t

        def output_gate(s, pre_t):
            o_t = work.tile([P, PACK, P], F32)
            for t in range(PACK):
                nc.scalar.activation(
                    out=o_t[:, t, :], in_=pre_t[:, t, :], func=ACT.Sigmoid, bias=bo_col[:, t, s : s + 1]
                )
            return o_t

        def gating_product(s, o_t):
            hn_grouped = work.tile([P, P, PACK], BF16, align_bytes=64)
            nc.vector.tensor_mul(
                out=hn_grouped[:], in0=o_t[:].rearrange("p t r -> p r t"), in1=tanh_c[:, s]
            )
            return hn_grouped

        def quantise_hn(s, hn_grouped):
            nc.vector.quantize_mx(
                out=hn_codes[:, s, :].bitcast(FP8X4),
                scales=hn_scales[:, s, :],
                in_=hn_grouped[:].rearrange("p r t -> p (r t)"),
            )

        def spread_by():
            by_flat = by_all[:].rearrange("p s m -> p (s m)")
            for bank in range(2):
                by_ps = psum.tile([P, 2 * FEAT], BF16, tag="xh_t")
                for part in range(2):
                    cols = slice(FEAT * (2 * bank + part), FEAT * (2 * bank + part + 1))
                    nc.tensor.matmul(
                        out=by_ps[:, FEAT * part : FEAT * (part + 1)],
                        lhsT=ones[:],
                        rhs=by_row[:, cols],
                        start=True,
                        stop=True,
                    )
                nc.vector.tensor_copy(out=by_flat[:, 2 * FEAT * bank : 2 * FEAT * (bank + 1)], in_=by_ps[:])

        def second_product(pair):
            acc = psum.tile([P, PAIR, OUT], F32, tag=("xh_t" if pair < 2 else "c_t"))
            for j in range(PAIR):
                s = PAIR * pair + j
                nc.tensor.matmul_mx(
                    out=acc[:, j, :],
                    lhsT=hn_codes[:, s, :].bitcast(FP8X4),
                    lhsT_scale=hn_scales[:, s, :],
                    rhs=wy_words[:, s, :].bitcast(FP8X4),
                    rhs_scale=wy_planes[:, s, :],
                    start=True,
                    stop=True,
                )
            return acc

        def finish(pair, acc):
            streams = slice(PAIR * pair, PAIR * (pair + 1))
            nc.vector.tensor_add(out=y_sb[:, streams, :], in0=acc[:], in1=by_all[:, streams, :])
            nc.sync.dma_start(
                out=out[:, PAIR * OUT * pair : PAIR * OUT * (pair + 1)],
                in_=y_sb[:, streams, :].rearrange("p s m -> p (s m)"),
            )

        def turn_bo():
            bo_t = psum.tile([P, HALVES, P], F32, tag="c_t")
            transpose_words(bo_t, bo_rows, 0)
            nc.vector.tensor_copy(
                out=bo_col[:].rearrange("p (u e) s -> p u e s", e=2),
                in_=bo_t[:].bitcast(BF16).rearrange("p u (s e) -> p u e s", e=2)[:, :, :, 0:STREAMS],
            )

        pre_of = {}
        gate_of = {}
        xh_of = {}
        hn_of = {}

        def live(s):
            return 0 <= s < STREAMS

        def multiply(s):
            pre_of[s] = leave_psum(first_product(s))

        def gate(s):
            gate_of[s] = output_gate(s, turn_pre(pre_of[s]))

        for period in range(-1, STREAMS // PAIR - 1):
            a = PAIR * period
            b = a + 1
            n0 = a + 2
            n1 = a + 3
            if live(a):
                multiply(a)
            if period == 0:
                turn_bo()
            if live(a - 1):
                gate(a - 1)
            if live(n0):
                xh_of[n0] = turn_xh(n0)
                xh_of[n1] = turn_xh(n1)
            if live(a):
                gate(a)
            if live(a - 1):
                hn_of[a - 1] = gating_product(a - 1, gate_of[a - 1])
            if live(n0):
                c_t0 = turn_c(n0)
                c_t1 = turn_c(n1)
                tanh_of_c(n0, c_t0)
                quantise_xh(n0, xh_of[n0])
                quantise_xh(n1, xh_of[n1])
            if live(a - 1):
                quantise_hn(a - 1, hn_of[a - 1])
            if period == 0:
                spread_by()
            if live(n0):
                if live(b):
                    multiply(b)
                tanh_of_c(n1, c_t1)
            if live(a):
                hn_of[a] = gating_product(a, gate_of[a])
                quantise_hn(a, hn_of[a])
        multiply(6)
        gate(5)
        multiply(7)
        gate(6)
        hn_of[5] = gating_product(5, gate_of[5])
        finish(0, second_product(0))
        quantise_hn(5, hn_of[5])
        hn_of[6] = gating_product(6, gate_of[6])
        gate(7)
        hn_of[7] = gating_product(7, gate_of[7])
        quantise_hn(6, hn_of[6])
        quantise_hn(7, hn_of[7])
        for pair in range(1, STREAMS // PAIR):
            finish(pair, second_product(pair))
